import numpy as np
import ml_dtypes


def mxq(x, axis, fmt="e4m3"):
    dtype, down = {"e4m3": (ml_dtypes.float8_e4m3fn, 7), "e5m2": (ml_dtypes.float8_e5m2, 14)}[fmt]
    v = np.moveaxis(np.asarray(x, np.float32).astype(ml_dtypes.bfloat16).astype(np.float64), axis, -1)
    blocks = v.reshape(v.shape[:-1] + (-1, 32))
    amax = np.abs(blocks).max(-1, keepdims=True)
    byte = np.maximum(np.where(amax > 0, np.frexp(amax)[1] - 1 + 127, 0) - down, 1)
    scale = np.exp2(byte - 127.0)
    codes = (blocks / scale).astype(np.float32).astype(dtype).astype(np.float64)
    return np.moveaxis((codes * scale).reshape(v.shape), -1, axis)


WIDE = False


def mx_kscale(k):
    if not WIDE:
        return np.ones(k)
    levels = np.array([10, -10, 5, -5, 0])
    a = np.random.permutation(np.resize(levels, k // 512 * 4)).reshape(k // 512, 4)
    idx = np.arange(k)
    return np.exp2(a[idx // 512, idx % 128 // 32])


BF16 = ml_dtypes.bfloat16


def bf(x):
    return np.asarray(x, np.float32).astype(BF16)


def f64(x):
    return np.asarray(x).astype(np.float64)


E2M1 = np.array([0.0, 0.5, 1.0, 1.5, 2.0, 3.0, 4.0, 6.0, -0.0, -0.5, -1.0, -1.5, -2.0, -3.0, -4.0, -6.0])


def pack_weight(w, fmt):
    k, n = w.shape
    w = f64(bf(w)).reshape(k // 32, 32, n)
    amax = np.abs(w).max(1)
    if fmt == "e4m3":
        byte = np.frexp(amax)[1] - 1 + 127 - 7
    else:
        mant, ex = np.frexp(amax / 6.0)
        byte = np.where(mant > 0.5, ex, ex - 1) + 127
    byte = np.clip(np.where(amax > 0, byte, 1), 1, 254)
    scaled = (w * np.exp2(127.0 - byte)[:, None, :]).reshape(k, n).astype(np.float32)
    by_word = np.ascontiguousarray(scaled.reshape(k // 512, 128, 4, n).transpose(0, 1, 3, 2))
    if fmt == "e4m3":
        words = by_word.astype(ml_dtypes.float8_e4m3fn).view(np.uint8)
    else:
        c = by_word.astype(ml_dtypes.float4_e2m1fn).view(np.uint8) & 0xF
        words = c[..., 0::2] | (c[..., 1::2] << 4)
    return np.ascontiguousarray(words), np.ascontiguousarray(byte.astype(np.uint8).reshape(k // 512, 16, n))


def unpack_weight(words, scales, fmt):
    g, p, n, _ = words.shape
    if fmt == "e4m3":
        vals = np.ascontiguousarray(words).view(ml_dtypes.float8_e4m3fn).astype(np.float64)
    else:
        nib = np.empty((g, p, n, 4), np.uint8)
        nib[..., 0::2] = words & 0xF
        nib[..., 1::2] = words >> 4
        vals = E2M1[nib]
    vals = vals * np.repeat(np.exp2(scales.astype(np.float64) - 127.0), 8, axis=1)[..., None]
    return vals.transpose(0, 1, 3, 2).reshape(g * 512, n)


N, IN_DIM, HID, OUT_DIM = 512, 16384, 512, 256


def setup_inputs():
    s = mx_kscale(IN_DIM)
    X = bf(np.random.standard_normal((N, IN_DIM)) * s)
    A = bf(np.random.uniform(0.0, 1.0, (N, N)) * 0.5 / np.sqrt(N))
    W_in_words, W_in_scales = pack_weight(np.random.standard_normal((IN_DIM, HID)) / np.sqrt(IN_DIM) / s[:, None], "e4m3")
    b_in = bf(np.random.standard_normal(HID) * 0.1)
    eps0 = bf(np.random.uniform(0.2, 0.4, (1,)))
    return {"X": X,
            "A": A,
            "W_in_words": W_in_words,
            "W_in_scales": W_in_scales,
            "b_in": b_in,
            "eps0": eps0}


def reference(X, A, W_in_words, W_in_scales, b_in, eps0):
    h = (mxq(f64(X), 1, "e4m3") @ unpack_weight(W_in_words, W_in_scales, "e4m3")) + f64(b_in)
    return (mxq(f64(A), 1, "e4m3") @ mxq(h, 0, "e4m3")) + (1.0 + f64(eps0)) * h

@@ -1,0 +1,208 @@
+from contextlib import ExitStack
+
+import concourse.mybir as mybir
+from concourse.masks import make_identity
+
+F32 = mybir.dt.float32
+BF16 = mybir.dt.bfloat16
+I32 = mybir.dt.int32
+U32 = mybir.dt.uint32
+U8 = mybir.dt.uint8
+FP8X4 = mybir.dt.float8_e4m3fn_x4
+ADD = mybir.AluOpType.add
+MULT = mybir.AluOpType.mult
+
+P = 128
+PACK = 4
+GROUP = P * PACK
+HALVES = 2
+NODES = 512
+IN_DIM = 16384
+HID = 512
+TILES = NODES // P
+GROUPS = IN_DIM // GROUP
+CHUNK_GROUPS = 4
+CHUNKS = GROUPS // CHUNK_GROUPS
+CHUNK_K = CHUNK_GROUPS * GROUP
+X_BUFS = 4
+RUN = 2
+ROUNDS = GROUPS // RUN
+EPS_COLS = 32
+
+FLOPS = 2 * NODES * IN_DIM * HID + 2 * NODES * NODES * HID
+
+
+def tile_gin_pa_k_kernel(tc, X, A, W_in_words, W_in_scales, b_in, eps0, out):
+    nc = tc.nc
+
+    x_rows = X.rearrange("(r t) k -> r t k", t=TILES)
+    a_rows = A.rearrange("(r t) j -> r t j", t=TILES)
+    out_rows = out.rearrange("(r t) n -> r t n", t=TILES)
+    w_words = W_in_words.rearrange("g p n t -> p g (n t)").bitcast(I32)
+    w_scales = W_in_scales.rearrange("(c j) (q s) n -> j q s c n", j=CHUNK_GROUPS, s=4).bitcast(I32)
+
+    with ExitStack() as stack:
+        stack.enter_context(tc.manual_schedule())
+        const = stack.enter_context(tc.tile_pool(name="const", bufs=1))
+        x_pool = stack.enter_context(tc.tile_pool(name="x", bufs=X_BUFS))
+        w_pool = stack.enter_context(tc.tile_pool(name="w", bufs=CHUNKS))
+        work = stack.enter_context(tc.tile_pool(name="work", bufs=2 * RUN))
+        acc_pool = stack.enter_context(tc.psum_pool(name="acc", bufs=1))
+        bank_pool = stack.enter_context(tc.psum_pool(name="bank", bufs=4))
+
+        w_planes = const.tile([P, CHUNKS, HID], U8, align_bytes=64)
+        nc.vector.memset(w_planes[:].bitcast(I32), 0)
+        first_row = const.tile([P, HID + EPS_COLS], BF16)
+        nc.vector.memset(first_row[:], 0.0)
+        ones = const.tile([P, P], BF16)
+        nc.vector.memset(ones[:], 1.0)
+        ident = const.tile([P, P], F32)
+        make_identity(nc, ident[:])
+        nc.scalar.dma_start(out=first_row[0:1, 0:HID], in_=b_in.unsqueeze(0))
+        nc.scalar.dma_start(out=first_row[0:1, HID : HID + 1], in_=eps0.unsqueeze(0))
+
+        rows_of = {}
+        w_of = {}
+
+        def load_scale_planes():
+            for j in range(CHUNK_GROUPS):
+                for q in range(4):
+                    top = 32 * q + 4 * j
+                    nc.sync.dma_start(out=w_planes[top : top + 4, :, :].bitcast(I32), in_=w_scales[j, q])
+
+        def load_chunk(c):
+            x_chunk = x_pool.tile([P, TILES, CHUNK_K], BF16, name="x_chunk")
+            pieces = CHUNK_GROUPS if c == 0 else 1
+            width = CHUNK_K // pieces
+            for i in range(pieces):
+                nc.sync.dma_start(
+                    out=x_chunk[:, :, i * width : (i + 1) * width],
+                    in_=x_rows[:, :, c * CHUNK_K + i * width : c * CHUNK_K + (i + 1) * width],
+                )
+            if c == 0:
+                load_scale_planes()
+            w_chunk = w_pool.tile([P, CHUNK_GROUPS, HID], U32, align_bytes=64, name="w_chunk")
+            nc.sync.dma_start(
+                out=w_chunk[:].bitcast(I32), in_=w_words[:, c * CHUNK_GROUPS : (c + 1) * CHUNK_GROUPS, :]
+            )
+            x_words = x_chunk[:].bitcast(F32)
+            for i in range(CHUNK_GROUPS):
+                rows_of[c * CHUNK_GROUPS + i] = x_words[:, :, i * GROUP // 2 : (i + 1) * GROUP // 2]
+                w_of[c * CHUNK_GROUPS + i] = w_chunk[:, i, :]
+
+        def load_a():
+            a_sb = const.tile([P, TILES, NODES], BF16)
+            nc.sync.dma_start(out=a_sb[:], in_=a_rows)
+            rows_of[GROUPS] = a_sb[:].bitcast(F32)
+
+        items_of_round = [list(range(s, min(s + RUN, GROUPS + 1))) for s in range(0, GROUPS + 1, RUN)]
+        sorted_of = {}
+        grouped_of = {}
+        codes_of = {}
+        planes_of = {}
+
+        def sort_round(r):
+            for g in items_of_round[r]:
+                sorted_words = work.tile([P, TILES, HALVES, P], F32, name="sorted_words")
+                nc.vector.tensor_copy(
+                    out=sorted_words[:], in_=rows_of[g].rearrange("r t (p u) -> r t u p", u=HALVES)
+                )
+                sorted_of[g] = sorted_words
+                next_chunk = g // CHUNK_GROUPS + X_BUFS
+                if (g + 1) % CHUNK_GROUPS == 0 and next_chunk < CHUNKS:
+                    load_chunk(next_chunk)
+                    if next_chunk == CHUNKS - 1:
+                        load_a()
+
+        def transpose_round(r):
+            for g in items_of_round[r]:
+                grouped = work.tile([P, TILES * P * PACK], BF16, align_bytes=64, name="grouped")
+                grouped_words = grouped[:].bitcast(F32).rearrange("p (t r u) -> p t r u", t=TILES, u=HALVES)
+                for first in range(0, TILES, 2):
+                    bank = bank_pool.tile([P, 2, HALVES, P], F32, name="bank")
+                    for i in range(2):
+                        for u in range(HALVES):
+                            nc.tensor.transpose(bank[:, i, u, :], sorted_of[g][:, first + i, u, :], ident[:])
+                    nc.scalar.copy(
+                        out=grouped_words[:, first : first + 2, :, :],
+                        in_=bank[:].rearrange("p t u r -> p t r u"),
+                    )
+                grouped_of[g] = grouped
+
+        def quantise_round(r):
+            for g in items_of_round[r]:
+                codes = work.tile([P, TILES, P], U32, align_bytes=64, name="codes")
+                planes = work.tile([P, TILES, P], U8, align_bytes=64, name="planes")
+                nc.vector.quantize_mx(
+                    out=codes[:].rearrange("p t r -> p (t r)").bitcast(FP8X4),
+                    scales=planes[:].rearrange("p t r -> p (t r)"),
+                    in_=grouped_of[g][:],
+                )
+                codes_of[g] = codes
+                planes_of[g] = planes
+
+        acc = [acc_pool.tile([P, HID], F32, name="acc%d" % t) for t in range(TILES)]
+
+        def multiply_round(r):
+            for t in range(TILES):
+                for g in items_of_round[r]:
+                    nc.tensor.matmul_mx(
+                        out=acc[t][:],
+                        lhsT=codes_of[g][:, t, :].bitcast(FP8X4),
+                        lhsT_scale=planes_of[g][:, t, :],
+                        rhs=w_of[g].bitcast(FP8X4),
+                        rhs_scale=w_planes[4 * (g % CHUNK_GROUPS) : P, g // CHUNK_GROUPS, :],
+                        start=(g == 0),
+                        stop=(g == GROUPS - 1),
+                    )
+
+        for c in range(X_BUFS):
+            load_chunk(c)
+
+        spread_b = bank_pool.tile([P, HID], F32, name="spread_b", tag="bank")
+        nc.tensor.matmul(out=spread_b[:], lhsT=ones[:], rhs=first_row[:, 0:HID], start=True, stop=True)
+        spread_eps = bank_pool.tile([P, EPS_COLS], F32, name="spread_eps", tag="bank")
+        nc.tensor.matmul(out=spread_eps[:], lhsT=ones[:], rhs=first_row[:, HID:], start=True, stop=True)
+        bias = const.tile([P, HID], F32)
+        nc.scalar.copy(out=bias[:], in_=spread_b[:])
+        one_plus_eps = const.tile([P, 1], F32)
+        nc.vector.tensor_scalar_add(out=one_plus_eps[:], in0=spread_eps[:, 0:1], scalar1=1.0)
+
+        sort_round(0)
+        transpose_round(0)
+        sort_round(1)
+        for r in range(ROUNDS + 1):
+            if r + 1 <= ROUNDS:
+                transpose_round(r + 1)
+            quantise_round(r)
+            if r + 2 <= ROUNDS:
+                sort_round(r + 2)
+            if r < ROUNDS:
+                multiply_round(r)
+
+        h = const.tile([P, TILES, HID], F32)
+        for t in range(TILES):
+            nc.vector.tensor_tensor(out=h[:, t, :], in0=acc[t][:], in1=bias[:], op=ADD)
+        h_grouped = const.tile([P, HID, PACK], BF16, align_bytes=64)
+        nc.vector.tensor_copy(out=h_grouped[:], in_=h[:].rearrange("r t n -> r n t"))
+        h_codes = const.tile([P, HID], U32, align_bytes=64)
+        h_planes = const.tile([P, HID], U8, align_bytes=64)
+        nc.vector.quantize_mx(
+            out=h_codes[:].bitcast(FP8X4), scales=h_planes[:], in_=h_grouped[:].rearrange("r n t -> r (n t)")
+        )
+        result = const.tile([P, TILES, HID], F32)
+        for t in range(TILES):
+            gathered = bank_pool.tile([P, HID], F32, name="gathered", tag="bank")
+            nc.tensor.matmul_mx(
+                out=gathered[:],
+                lhsT=codes_of[GROUPS][:, t, :].bitcast(FP8X4),
+                lhsT_scale=planes_of[GROUPS][:, t, :],
+                rhs=h_codes[:].bitcast(FP8X4),
+                rhs_scale=h_planes[:],
+                start=True,
+                stop=True,
+            )
+            nc.vector.scalar_tensor_tensor(
+                out=result[:, t, :], in0=h[:, t, :], scalar=one_plus_eps[:, 0:1], in1=gathered[:], op0=MULT, op1=ADD
+            )
+            nc.sync.dma_start(out=out_rows[:, t, :], in_=result[:, t, :])

@@ -39,7 +39,7 @@ def tile_gin_pa_k_kernel(tc, X, A, W_in_words, W_in_scales, b_in, eps0, out):
     a_rows = A.rearrange("(r t) j -> r t j", t=TILES)
     out_rows = out.rearrange("(r t) n -> r t n", t=TILES)
     w_words = W_in_words.rearrange("g p n t -> p g (n t)").bitcast(I32)
-    w_scales = W_in_scales.rearrange("(c j) (q s) n -> j q s c n", j=CHUNK_GROUPS, s=4).bitcast(I32)
+    w_scales = W_in_scales.rearrange("(c j) (q s) n -> c q j s n", j=CHUNK_GROUPS, s=4).bitcast(I32)
 
     with ExitStack() as stack:
         stack.enter_context(tc.manual_schedule())
@@ -64,12 +64,6 @@ def tile_gin_pa_k_kernel(tc, X, A, W_in_words, W_in_scales, b_in, eps0, out):
         rows_of = {}
         w_of = {}
 
-        def load_scale_planes():
-            for j in range(CHUNK_GROUPS):
-                for q in range(4):
-                    top = 32 * q + 4 * j
-                    nc.sync.dma_start(out=w_planes[top : top + 4, :, :].bitcast(I32), in_=w_scales[j, q])
-
         def load_chunk(c):
             x_chunk = x_pool.tile([P, TILES, CHUNK_K], BF16, name="x_chunk")
             pieces = CHUNK_GROUPS if c == 0 else 1
@@ -79,8 +73,8 @@ def tile_gin_pa_k_kernel(tc, X, A, W_in_words, W_in_scales, b_in, eps0, out):
                     out=x_chunk[:, :, i * width : (i + 1) * width],
                     in_=x_rows[:, :, c * CHUNK_K + i * width : c * CHUNK_K + (i + 1) * width],
                 )
-            if c == 0:
-                load_scale_planes()
+            for q in range(4):
+                nc.sync.dma_start(out=w_planes[32 * q : 32 * q + 16, c, :].bitcast(I32), in_=w_scales[c, q])
             w_chunk = w_pool.tile([P, CHUNK_GROUPS, HID], U32, align_bytes=64, name="w_chunk")
             nc.sync.dma_start(
                 out=w_chunk[:].bitcast(I32), in_=w_words[:, c * CHUNK_GROUPS : (c + 1) * CHUNK_GROUPS, :]

@@ -24,9 +24,10 @@ GROUPS = IN_DIM // GROUP
 CHUNK_GROUPS = 4
 CHUNKS = GROUPS // CHUNK_GROUPS
 CHUNK_K = CHUNK_GROUPS * GROUP
-X_BUFS = 4
+ITEMS = CHUNKS * TILES
 RUN = 2
-ROUNDS = GROUPS // RUN
+ROUNDS = ITEMS // RUN
+X_BUFS = 8
 EPS_COLS = 32
 
 FLOPS = 2 * NODES * IN_DIM * HID + 2 * NODES * NODES * HID
@@ -64,94 +65,102 @@ def tile_gin_pa_k_kernel(tc, X, A, W_in_words, W_in_scales, b_in, eps0, out):
         rows_of = {}
         w_of = {}
 
-        def load_chunk(c):
-            x_chunk = x_pool.tile([P, TILES, CHUNK_K], BF16, name="x_chunk")
-            pieces = CHUNK_GROUPS if c == 0 else 1
-            width = CHUNK_K // pieces
-            for i in range(pieces):
-                nc.sync.dma_start(
-                    out=x_chunk[:, :, i * width : (i + 1) * width],
-                    in_=x_rows[:, :, c * CHUNK_K + i * width : c * CHUNK_K + (i + 1) * width],
-                )
+        def load_round(r):
+            c, half = divmod(r, TILES // RUN)
+            x_pair = x_pool.tile([P, RUN, CHUNK_K], BF16, name="x_pair")
+            nc.sync.dma_start(
+                out=x_pair[:], in_=x_rows[:, half * RUN : (half + 1) * RUN, c * CHUNK_K : (c + 1) * CHUNK_K]
+            )
+            x_words = x_pair[:].bitcast(F32)
+            for i in range(RUN):
+                rows_of[r * RUN + i] = x_words[:, i, :].rearrange("r (g w) -> r g w", g=CHUNK_GROUPS)
+            if half == TILES // RUN - 1:
+                load_w(c)
+
+        def load_w(c):
             for q in range(4):
                 nc.sync.dma_start(out=w_planes[32 * q : 32 * q + 16, c, :].bitcast(I32), in_=w_scales[c, q])
             w_chunk = w_pool.tile([P, CHUNK_GROUPS, HID], U32, align_bytes=64, name="w_chunk")
             nc.sync.dma_start(
                 out=w_chunk[:].bitcast(I32), in_=w_words[:, c * CHUNK_GROUPS : (c + 1) * CHUNK_GROUPS, :]
             )
-            x_words = x_chunk[:].bitcast(F32)
-            for i in range(CHUNK_GROUPS):
-                rows_of[c * CHUNK_GROUPS + i] = x_words[:, :, i * GROUP // 2 : (i + 1) * GROUP // 2]
-                w_of[c * CHUNK_GROUPS + i] = w_chunk[:, i, :]
+            w_of[c] = w_chunk
 
         def load_a():
             a_sb = const.tile([P, TILES, NODES], BF16)
             nc.sync.dma_start(out=a_sb[:], in_=a_rows)
-            rows_of[GROUPS] = a_sb[:].bitcast(F32)
+            rows_of[ITEMS] = a_sb[:].bitcast(F32)
 
-        items_of_round = [list(range(s, min(s + RUN, GROUPS + 1))) for s in range(0, GROUPS + 1, RUN)]
+        items_of_round = [list(range(s, min(s + RUN, ITEMS + 1))) for s in range(0, ITEMS + 1, RUN)]
         sorted_of = {}
         grouped_of = {}
         codes_of = {}
         planes_of = {}
 
         def sort_round(r):
-            for g in items_of_round[r]:
-                sorted_words = work.tile([P, TILES, HALVES, P], F32, name="sorted_words")
+            for item in items_of_round[r]:
+                sorted_words = work.tile([P, PACK, HALVES, P], F32, name="sorted_words")
                 nc.vector.tensor_copy(
-                    out=sorted_words[:], in_=rows_of[g].rearrange("r t (p u) -> r t u p", u=HALVES)
+                    out=sorted_words[:], in_=rows_of[item].rearrange("r n (p u) -> r n u p", u=HALVES)
                 )
-                sorted_of[g] = sorted_words
-                next_chunk = g // CHUNK_GROUPS + X_BUFS
-                if (g + 1) % CHUNK_GROUPS == 0 and next_chunk < CHUNKS:
-                    load_chunk(next_chunk)
-                    if next_chunk == CHUNKS - 1:
-                        load_a()
+                sorted_of[item] = sorted_words
+            if r + X_BUFS < ROUNDS:
+                load_round(r + X_BUFS)
+            if r + X_BUFS == ROUNDS - 1:
+                load_a()
 
         def transpose_round(r):
-            for g in items_of_round[r]:
-                grouped = work.tile([P, TILES * P * PACK], BF16, align_bytes=64, name="grouped")
-                grouped_words = grouped[:].bitcast(F32).rearrange("p (t r u) -> p t r u", t=TILES, u=HALVES)
-                for first in range(0, TILES, 2):
+            for item in items_of_round[r]:
+                grouped = work.tile([P, PACK * P * PACK], BF16, align_bytes=64, name="grouped")
+                grouped_words = grouped[:].bitcast(F32).rearrange("p (n r u) -> p n r u", n=PACK, u=HALVES)
+                for first in range(0, PACK, 2):
                     bank = bank_pool.tile([P, 2, HALVES, P], F32, name="bank")
                     for i in range(2):
                         for u in range(HALVES):
-                            nc.tensor.transpose(bank[:, i, u, :], sorted_of[g][:, first + i, u, :], ident[:])
+                            nc.tensor.transpose(bank[:, i, u, :], sorted_of[item][:, first + i, u, :], ident[:])
                     nc.scalar.copy(
                         out=grouped_words[:, first : first + 2, :, :],
-                        in_=bank[:].rearrange("p t u r -> p t r u"),
+                        in_=bank[:].rearrange("p n u r -> p n r u"),
                     )
-                grouped_of[g] = grouped
+                grouped_of[item] = grouped
 
         def quantise_round(r):
-            for g in items_of_round[r]:
-                codes = work.tile([P, TILES, P], U32, align_bytes=64, name="codes")
-                planes = work.tile([P, TILES, P], U8, align_bytes=64, name="planes")
+            for item in items_of_round[r]:
+                codes = work.tile([P, PACK, P], U32, align_bytes=64, name="codes")
+                planes = work.tile([P, PACK, P], U8, align_bytes=64, name="planes")
                 nc.vector.quantize_mx(
-                    out=codes[:].rearrange("p t r -> p (t r)").bitcast(FP8X4),
-                    scales=planes[:].rearrange("p t r -> p (t r)"),
-                    in_=grouped_of[g][:],
+                    out=codes[:].rearrange("p n r -> p (n r)").bitcast(FP8X4),
+                    scales=planes[:].rearrange("p n r -> p (n r)"),
+                    in_=grouped_of[item][:],
                 )
-                codes_of[g] = codes
-                planes_of[g] = planes
+                codes_of[item] = codes
+                planes_of[item] = planes
 
         acc = [acc_pool.tile([P, HID], F32, name="acc%d" % t) for t in range(TILES)]
+        h = const.tile([P, TILES, HID], F32)
 
         def multiply_round(r):
-            for t in range(TILES):
-                for g in items_of_round[r]:
+            for item in items_of_round[r]:
+                c, t = divmod(item, TILES)
+                for j in range(CHUNK_GROUPS):
                     nc.tensor.matmul_mx(
                         out=acc[t][:],
-                        lhsT=codes_of[g][:, t, :].bitcast(FP8X4),
-                        lhsT_scale=planes_of[g][:, t, :],
-                        rhs=w_of[g].bitcast(FP8X4),
-                        rhs_scale=w_planes[4 * (g % CHUNK_GROUPS) : P, g // CHUNK_GROUPS, :],
-                        start=(g == 0),
-                        stop=(g == GROUPS - 1),
+                        lhsT=codes_of[item][:, j, :].bitcast(FP8X4),
+                        lhsT_scale=planes_of[item][:, j, :],
+                        rhs=w_of[c][:, j, :].bitcast(FP8X4),
+                        rhs_scale=w_planes[4 * j : P, c, :],
+                        start=(c == 0 and j == 0),
+                        stop=(c == CHUNKS - 1 and j == CHUNK_GROUPS - 1),
                     )
 
-        for c in range(X_BUFS):
-            load_chunk(c)
+        def add_bias_round(r):
+            for item in items_of_round[r]:
+                c, t = divmod(item, TILES)
+                if c == CHUNKS - 1:
+                    nc.vector.tensor_tensor(out=h[:, t, :], in0=acc[t][:], in1=bias[:], op=ADD)
+
+        for r in range(X_BUFS):
+            load_round(r)
 
         spread_b = bank_pool.tile([P, HID], F32, name="spread_b", tag="bank")
         nc.tensor.matmul(out=spread_b[:], lhsT=ones[:], rhs=first_row[:, 0:HID], start=True, stop=True)
@@ -169,14 +178,13 @@ def tile_gin_pa_k_kernel(tc, X, A, W_in_words, W_in_scales, b_in, eps0, out):
             if r + 1 <= ROUNDS:
                 transpose_round(r + 1)
             quantise_round(r)
+            if r >= 1:
+                add_bias_round(r - 1)
             if r + 2 <= ROUNDS:
                 sort_round(r + 2)
             if r < ROUNDS:
                 multiply_round(r)
 
-        h = const.tile([P, TILES, HID], F32)
-        for t in range(TILES):
-            nc.vector.tensor_tensor(out=h[:, t, :], in0=acc[t][:], in1=bias[:], op=ADD)
         h_grouped = const.tile([P, HID, PACK], BF16, align_bytes=64)
         nc.vector.tensor_copy(out=h_grouped[:], in_=h[:].rearrange("r t n -> r n t"))
         h_codes = const.tile([P, HID], U32, align_bytes=64)
@@ -189,8 +197,8 @@ def tile_gin_pa_k_kernel(tc, X, A, W_in_words, W_in_scales, b_in, eps0, out):
             gathered = bank_pool.tile([P, HID], F32, name="gathered", tag="bank")
             nc.tensor.matmul_mx(
                 out=gathered[:],
-                lhsT=codes_of[GROUPS][:, t, :].bitcast(FP8X4),
-                lhsT_scale=planes_of[GROUPS][:, t, :],
+                lhsT=codes_of[ITEMS][:, t, :].bitcast(FP8X4),
+                lhsT_scale=planes_of[ITEMS][:, t, :],
                 rhs=h_codes[:].bitcast(FP8X4),
                 rhs_scale=h_planes[:],
                 start=True,

@@ -92,37 +92,29 @@ def tile_gin_pa_k_kernel(tc, X, A, W_in_words, W_in_scales, b_in, eps0, out):
             rows_of[ITEMS] = a_sb[:].bitcast(F32)
 
         items_of_round = [list(range(s, min(s + RUN, ITEMS + 1))) for s in range(0, ITEMS + 1, RUN)]
-        sorted_of = {}
         grouped_of = {}
         codes_of = {}
         planes_of = {}
-
-        def sort_round(r):
-            for item in items_of_round[r]:
-                sorted_words = work.tile([P, PACK, HALVES, P], F32, name="sorted_words")
-                nc.vector.tensor_copy(
-                    out=sorted_words[:], in_=rows_of[item].rearrange("r n (p u) -> r n u p", u=HALVES)
-                )
-                sorted_of[item] = sorted_words
-            if r + X_BUFS < ROUNDS:
-                load_round(r + X_BUFS)
-            if r + X_BUFS == ROUNDS - 1:
-                load_a()
 
         def transpose_round(r):
             for item in items_of_round[r]:
                 grouped = work.tile([P, PACK * P * PACK], BF16, align_bytes=64, name="grouped")
                 grouped_words = grouped[:].bitcast(F32).rearrange("p (n r u) -> p n r u", n=PACK, u=HALVES)
+                by_half = rows_of[item].rearrange("r n (p u) -> r n u p", u=HALVES)
                 for first in range(0, PACK, 2):
                     bank = bank_pool.tile([P, 2, HALVES, P], F32, name="bank")
                     for i in range(2):
                         for u in range(HALVES):
-                            nc.tensor.transpose(bank[:, i, u, :], sorted_of[item][:, first + i, u, :], ident[:])
+                            nc.tensor.transpose(bank[:, i, u, :], by_half[:, first + i, u, :], ident[:])
                     nc.scalar.copy(
                         out=grouped_words[:, first : first + 2, :, :],
                         in_=bank[:].rearrange("p n u r -> p n r u"),
                     )
                 grouped_of[item] = grouped
+            if r + X_BUFS < ROUNDS:
+                load_round(r + X_BUFS)
+            if r + X_BUFS == ROUNDS - 1:
+                load_a()
 
         def quantise_round(r):
             for item in items_of_round[r]:
@@ -171,17 +163,13 @@ def tile_gin_pa_k_kernel(tc, X, A, W_in_words, W_in_scales, b_in, eps0, out):
         one_plus_eps = const.tile([P, 1], F32)
         nc.vector.tensor_scalar_add(out=one_plus_eps[:], in0=spread_eps[:, 0:1], scalar1=1.0)
 
-        sort_round(0)
         transpose_round(0)
-        sort_round(1)
         for r in range(ROUNDS + 1):
             if r + 1 <= ROUNDS:
                 transpose_round(r + 1)
             quantise_round(r)
             if r >= 1:
                 add_bias_round(r - 1)
-            if r + 2 <= ROUNDS:
-                sort_round(r + 2)
             if r < ROUNDS:
                 multiply_round(r)
 

@@ -27,7 +27,9 @@ CHUNK_K = CHUNK_GROUPS * GROUP
 ITEMS = CHUNKS * TILES
 RUN = 2
 ROUNDS = ITEMS // RUN
-X_BUFS = 8
+X_BUFS = 16
+W_LOADS = 2
+VECTOR_COLS = 2 * HID // 3 // 4 * 4
 EPS_COLS = 32
 
 FLOPS = 2 * NODES * IN_DIM * HID + 2 * NODES * NODES * HID
@@ -65,25 +67,24 @@ def tile_gin_pa_k_kernel(tc, X, A, W_in_words, W_in_scales, b_in, eps0, out):
         rows_of = {}
         w_of = {}
 
-        def load_round(r):
-            c, half = divmod(r, TILES // RUN)
-            x_pair = x_pool.tile([P, RUN, CHUNK_K], BF16, name="x_pair")
-            nc.sync.dma_start(
-                out=x_pair[:], in_=x_rows[:, half * RUN : (half + 1) * RUN, c * CHUNK_K : (c + 1) * CHUNK_K]
-            )
-            x_words = x_pair[:].bitcast(F32)
-            for i in range(RUN):
-                rows_of[r * RUN + i] = x_words[:, i, :].rearrange("r (g w) -> r g w", g=CHUNK_GROUPS)
-            if half == TILES // RUN - 1:
+        def load_item(item):
+            c, t = divmod(item, TILES)
+            x_item = x_pool.tile([P, CHUNK_K], BF16, name="x_item")
+            nc.sync.dma_start(out=x_item[:], in_=x_rows[:, t, c * CHUNK_K : (c + 1) * CHUNK_K])
+            rows_of[item] = x_item[:].bitcast(F32).rearrange("r (g w) -> r g w", g=CHUNK_GROUPS)
+            if t == TILES - 1:
                 load_w(c)
 
         def load_w(c):
             for q in range(4):
                 nc.sync.dma_start(out=w_planes[32 * q : 32 * q + 16, c, :].bitcast(I32), in_=w_scales[c, q])
             w_chunk = w_pool.tile([P, CHUNK_GROUPS, HID], U32, align_bytes=64, name="w_chunk")
-            nc.sync.dma_start(
-                out=w_chunk[:].bitcast(I32), in_=w_words[:, c * CHUNK_GROUPS : (c + 1) * CHUNK_GROUPS, :]
-            )
+            part = CHUNK_GROUPS // W_LOADS
+            for j in range(0, CHUNK_GROUPS, part):
+                nc.sync.dma_start(
+                    out=w_chunk[:, j : j + part, :].bitcast(I32),
+                    in_=w_words[:, c * CHUNK_GROUPS + j : c * CHUNK_GROUPS + j + part, :],
+                )
             w_of[c] = w_chunk
 
         def load_a():
@@ -92,29 +93,37 @@ def tile_gin_pa_k_kernel(tc, X, A, W_in_words, W_in_scales, b_in, eps0, out):
             rows_of[ITEMS] = a_sb[:].bitcast(F32)
 
         items_of_round = [list(range(s, min(s + RUN, ITEMS + 1))) for s in range(0, ITEMS + 1, RUN)]
+        sorted_of = {}
         grouped_of = {}
         codes_of = {}
         planes_of = {}
+
+        def sort_round(r):
+            for item in items_of_round[r]:
+                sorted_words = work.tile([P, PACK, HALVES, P], F32, name="sorted_words")
+                nc.vector.tensor_copy(
+                    out=sorted_words[:], in_=rows_of[item].rearrange("r n (p u) -> r n u p", u=HALVES)
+                )
+                sorted_of[item] = sorted_words
+                if item + X_BUFS < ITEMS:
+                    load_item(item + X_BUFS)
+                if item + X_BUFS == ITEMS - 1:
+                    load_a()
 
         def transpose_round(r):
             for item in items_of_round[r]:
                 grouped = work.tile([P, PACK * P * PACK], BF16, align_bytes=64, name="grouped")
                 grouped_words = grouped[:].bitcast(F32).rearrange("p (n r u) -> p n r u", n=PACK, u=HALVES)
-                by_half = rows_of[item].rearrange("r n (p u) -> r n u p", u=HALVES)
                 for first in range(0, PACK, 2):
                     bank = bank_pool.tile([P, 2, HALVES, P], F32, name="bank")
                     for i in range(2):
                         for u in range(HALVES):
-                            nc.tensor.transpose(bank[:, i, u, :], by_half[:, first + i, u, :], ident[:])
+                            nc.tensor.transpose(bank[:, i, u, :], sorted_of[item][:, first + i, u, :], ident[:])
                     nc.scalar.copy(
                         out=grouped_words[:, first : first + 2, :, :],
                         in_=bank[:].rearrange("p n u r -> p n r u"),
                     )
                 grouped_of[item] = grouped
-            if r + X_BUFS < ROUNDS:
-                load_round(r + X_BUFS)
-            if r + X_BUFS == ROUNDS - 1:
-                load_a()
 
         def quantise_round(r):
             for item in items_of_round[r]:
@@ -151,8 +160,8 @@ def tile_gin_pa_k_kernel(tc, X, A, W_in_words, W_in_scales, b_in, eps0, out):
                 if c == CHUNKS - 1:
                     nc.vector.tensor_tensor(out=h[:, t, :], in0=acc[t][:], in1=bias[:], op=ADD)
 
-        for r in range(X_BUFS):
-            load_round(r)
+        for item in range(X_BUFS):
+            load_item(item)
 
         spread_b = bank_pool.tile([P, HID], F32, name="spread_b", tag="bank")
         nc.tensor.matmul(out=spread_b[:], lhsT=ones[:], rhs=first_row[:, 0:HID], start=True, stop=True)
@@ -163,18 +172,24 @@ def tile_gin_pa_k_kernel(tc, X, A, W_in_words, W_in_scales, b_in, eps0, out):
         one_plus_eps = const.tile([P, 1], F32)
         nc.vector.tensor_scalar_add(out=one_plus_eps[:], in0=spread_eps[:, 0:1], scalar1=1.0)
 
+        sort_round(0)
         transpose_round(0)
+        sort_round(1)
         for r in range(ROUNDS + 1):
             if r + 1 <= ROUNDS:
                 transpose_round(r + 1)
             quantise_round(r)
             if r >= 1:
                 add_bias_round(r - 1)
+            if r + 2 <= ROUNDS:
+                sort_round(r + 2)
             if r < ROUNDS:
                 multiply_round(r)
 
         h_grouped = const.tile([P, HID, PACK], BF16, align_bytes=64)
-        nc.vector.tensor_copy(out=h_grouped[:], in_=h[:].rearrange("r t n -> r n t"))
+        h_by_column = h[:].rearrange("r t n -> r n t")
+        nc.vector.tensor_copy(out=h_grouped[:, :VECTOR_COLS, :], in_=h_by_column[:, :VECTOR_COLS, :])
+        nc.scalar.copy(out=h_grouped[:, VECTOR_COLS:, :], in_=h_by_column[:, VECTOR_COLS:, :])
         h_codes = const.tile([P, HID], U32, align_bytes=64)
         h_planes = const.tile([P, HID], U8, align_bytes=64)
         nc.vector.quantize_mx(

@@ -29,7 +29,8 @@ RUN = 2
 ROUNDS = ITEMS // RUN
 X_BUFS = 16
 W_LOADS = 2
-VECTOR_COLS = 2 * HID // 3 // 4 * 4
+HALF = HID // 2
+VECTOR_COLS = 2 * HALF // 3 // 4 * 4
 EPS_COLS = 32
 
 FLOPS = 2 * NODES * IN_DIM * HID + 2 * NODES * NODES * HID
@@ -61,8 +62,6 @@ def tile_gin_pa_k_kernel(tc, X, A, W_in_words, W_in_scales, b_in, eps0, out):
         nc.vector.memset(ones[:], 1.0)
         ident = const.tile([P, P], F32)
         make_identity(nc, ident[:])
-        nc.scalar.dma_start(out=first_row[0:1, 0:HID], in_=b_in.unsqueeze(0))
-        nc.scalar.dma_start(out=first_row[0:1, HID : HID + 1], in_=eps0.unsqueeze(0))
 
         rows_of = {}
         w_of = {}
@@ -157,20 +156,24 @@ def tile_gin_pa_k_kernel(tc, X, A, W_in_words, W_in_scales, b_in, eps0, out):
         def add_bias_round(r):
             for item in items_of_round[r]:
                 c, t = divmod(item, TILES)
-                if c == CHUNKS - 1:
+                if c == CHUNKS - 1 and t < TILES - 1:
                     nc.vector.tensor_tensor(out=h[:, t, :], in0=acc[t][:], in1=bias[:], op=ADD)
 
         for item in range(X_BUFS):
             load_item(item)
 
-        spread_b = bank_pool.tile([P, HID], F32, name="spread_b", tag="bank")
-        nc.tensor.matmul(out=spread_b[:], lhsT=ones[:], rhs=first_row[:, 0:HID], start=True, stop=True)
-        spread_eps = bank_pool.tile([P, EPS_COLS], F32, name="spread_eps", tag="bank")
-        nc.tensor.matmul(out=spread_eps[:], lhsT=ones[:], rhs=first_row[:, HID:], start=True, stop=True)
+        nc.sync.dma_start(out=first_row[0:1, 0:HID], in_=b_in.unsqueeze(0))
+        nc.sync.dma_start(out=first_row[0:1, HID : HID + 1], in_=eps0.unsqueeze(0))
         bias = const.tile([P, HID], F32)
-        nc.scalar.copy(out=bias[:], in_=spread_b[:])
         one_plus_eps = const.tile([P, 1], F32)
-        nc.vector.tensor_scalar_add(out=one_plus_eps[:], in0=spread_eps[:, 0:1], scalar1=1.0)
+
+        def spread_constants():
+            spread_b = bank_pool.tile([P, HID], F32, name="spread_b", tag="bank")
+            nc.tensor.matmul(out=spread_b[:], lhsT=ones[:], rhs=first_row[:, 0:HID], start=True, stop=True)
+            spread_eps = bank_pool.tile([P, EPS_COLS], F32, name="spread_eps", tag="bank")
+            nc.tensor.matmul(out=spread_eps[:], lhsT=ones[:], rhs=first_row[:, HID:], start=True, stop=True)
+            nc.scalar.copy(out=bias[:], in_=spread_b[:])
+            nc.vector.tensor_scalar_add(out=one_plus_eps[:], in0=spread_eps[:, 0:1], scalar1=1.0)
 
         sort_round(0)
         transpose_round(0)
@@ -185,29 +188,69 @@ def tile_gin_pa_k_kernel(tc, X, A, W_in_words, W_in_scales, b_in, eps0, out):
                 sort_round(r + 2)
             if r < ROUNDS:
                 multiply_round(r)
+            if r == ROUNDS // 2:
+                spread_constants()
 
         h_grouped = const.tile([P, HID, PACK], BF16, align_bytes=64)
         h_by_column = h[:].rearrange("r t n -> r n t")
-        nc.vector.tensor_copy(out=h_grouped[:, :VECTOR_COLS, :], in_=h_by_column[:, :VECTOR_COLS, :])
-        nc.scalar.copy(out=h_grouped[:, VECTOR_COLS:, :], in_=h_by_column[:, VECTOR_COLS:, :])
         h_codes = const.tile([P, HID], U32, align_bytes=64)
         h_planes = const.tile([P, HID], U8, align_bytes=64)
-        nc.vector.quantize_mx(
-            out=h_codes[:].bitcast(FP8X4), scales=h_planes[:], in_=h_grouped[:].rearrange("r n t -> r (n t)")
-        )
-        result = const.tile([P, TILES, HID], F32)
-        for t in range(TILES):
-            gathered = bank_pool.tile([P, HID], F32, name="gathered", tag="bank")
-            nc.tensor.matmul_mx(
-                out=gathered[:],
-                lhsT=codes_of[ITEMS][:, t, :].bitcast(FP8X4),
-                lhsT_scale=planes_of[ITEMS][:, t, :],
-                rhs=h_codes[:].bitcast(FP8X4),
-                rhs_scale=h_planes[:],
-                start=True,
-                stop=True,
+        result = const.tile([P, 2, TILES, HALF], F32)
+
+        def last_bias(wave):
+            cols = slice(wave * HALF, (wave + 1) * HALF)
+            nc.vector.tensor_tensor(
+                out=h[:, TILES - 1, cols], in0=acc[TILES - 1][:, cols], in1=bias[:, cols], op=ADD
             )
-            nc.vector.scalar_tensor_tensor(
-                out=result[:, t, :], in0=h[:, t, :], scalar=one_plus_eps[:, 0:1], in1=gathered[:], op0=MULT, op1=ADD
+
+        def regroup_h(wave):
+            split = wave * HALF + VECTOR_COLS
+            nc.vector.tensor_copy(
+                out=h_grouped[:, wave * HALF : split, :], in_=h_by_column[:, wave * HALF : split, :]
             )
-            nc.sync.dma_start(out=out_rows[:, t, :], in_=result[:, t, :])
+            nc.scalar.copy(
+                out=h_grouped[:, split : (wave + 1) * HALF, :], in_=h_by_column[:, split : (wave + 1) * HALF, :]
+            )
+
+        def quantise_h(wave):
+            cols = slice(wave * HALF, (wave + 1) * HALF)
+            nc.vector.quantize_mx(
+                out=h_codes[:, cols].bitcast(FP8X4),
+                scales=h_planes[:, cols],
+                in_=h_grouped[:, cols, :].rearrange("r n t -> r (n t)"),
+            )
+
+        def gather(wave):
+            cols = slice(wave * HALF, (wave + 1) * HALF)
+            for first in range(0, TILES, 2):
+                gathered = bank_pool.tile([P, 2, HALF], F32, name="gathered", tag="bank")
+                for i in range(2):
+                    nc.tensor.matmul_mx(
+                        out=gathered[:, i, :],
+                        lhsT=codes_of[ITEMS][:, first + i, :].bitcast(FP8X4),
+                        lhsT_scale=planes_of[ITEMS][:, first + i, :],
+                        rhs=h_codes[:, cols].bitcast(FP8X4),
+                        rhs_scale=h_planes[:, cols],
+                        start=True,
+                        stop=True,
+                    )
+                nc.vector.scalar_tensor_tensor(
+                    out=result[:, wave, first : first + 2, :],
+                    in0=h[:, first : first + 2, cols],
+                    scalar=one_plus_eps[:, 0:1],
+                    in1=gathered[:],
+                    op0=MULT,
+                    op1=ADD,
+                )
+                nc.sync.dma_start(
+                    out=out_rows[:, first : first + 2, cols], in_=result[:, wave, first : first + 2, :]
+                )
+
+        last_bias(0)
+        regroup_h(0)
+        last_bias(1)
+        quantise_h(0)
+        regroup_h(1)
+        quantise_h(1)
+        gather(0)
+        gather(1)

from contextlib import ExitStack

import concourse.mybir as mybir
from concourse.masks import make_identity

F32 = mybir.dt.float32
BF16 = mybir.dt.bfloat16
I32 = mybir.dt.int32
U32 = mybir.dt.uint32
U8 = mybir.dt.uint8
FP8X4 = mybir.dt.float8_e4m3fn_x4
ADD = mybir.AluOpType.add
MULT = mybir.AluOpType.mult

P = 128
PACK = 4
GROUP = P * PACK
HALVES = 2
NODES = 512
IN_DIM = 16384
HID = 512
TILES = NODES // P
GROUPS = IN_DIM // GROUP
CHUNK_GROUPS = 4
CHUNKS = GROUPS // CHUNK_GROUPS
CHUNK_K = CHUNK_GROUPS * GROUP
ITEMS = CHUNKS * TILES
RUN = 2
ROUNDS = ITEMS // RUN
X_BUFS = 16
W_LOADS = 2
HALF = HID // 2
VECTOR_COLS = 2 * HALF // 3 // 4 * 4
EPS_COLS = 32

FLOPS = 2 * NODES * IN_DIM * HID + 2 * NODES * NODES * HID


def tile_gin_pa_k_kernel(tc, X, A, W_in_words, W_in_scales, b_in, eps0, out):
    nc = tc.nc

    x_rows = X.rearrange("(r t) k -> r t k", t=TILES)
    a_rows = A.rearrange("(r t) j -> r t j", t=TILES)
    out_rows = out.rearrange("(r t) n -> r t n", t=TILES)
    w_words = W_in_words.rearrange("g p n t -> p g (n t)").bitcast(I32)
    w_scales = W_in_scales.rearrange("(c j) (q s) n -> c q j s n", j=CHUNK_GROUPS, s=4).bitcast(I32)

    with ExitStack() as stack:
        stack.enter_context(tc.manual_schedule())
        const = stack.enter_context(tc.tile_pool(name="const", bufs=1))
        x_pool = stack.enter_context(tc.tile_pool(name="x", bufs=X_BUFS))
        w_pool = stack.enter_context(tc.tile_pool(name="w", bufs=CHUNKS))
        work = stack.enter_context(tc.tile_pool(name="work", bufs=2 * RUN))
        acc_pool = stack.enter_context(tc.psum_pool(name="acc", bufs=1))
        bank_pool = stack.enter_context(tc.psum_pool(name="bank", bufs=4))

        w_planes = const.tile([P, CHUNKS, HID], U8, align_bytes=64)
        nc.vector.memset(w_planes[:].bitcast(I32), 0)
        first_row = const.tile([P, HID + EPS_COLS], BF16)
        nc.vector.memset(first_row[:], 0.0)
        ones = const.tile([P, P], BF16)
        nc.vector.memset(ones[:], 1.0)
        ident = const.tile([P, P], F32)
        make_identity(nc, ident[:])

        rows_of = {}
        w_of = {}

        def load_item(item):
            c, t = divmod(item, TILES)
            x_item = x_pool.tile([P, CHUNK_K], BF16, name="x_item")
            nc.sync.dma_start(out=x_item[:], in_=x_rows[:, t, c * CHUNK_K : (c + 1) * CHUNK_K])
            rows_of[item] = x_item[:].bitcast(F32).rearrange("r (g w) -> r g w", g=CHUNK_GROUPS)
            if t == TILES - 1:
                load_w(c)

        def load_w(c):
            for q in range(4):
                nc.sync.dma_start(out=w_planes[32 * q : 32 * q + 16, c, :].bitcast(I32), in_=w_scales[c, q])
            w_chunk = w_pool.tile([P, CHUNK_GROUPS, HID], U32, align_bytes=64, name="w_chunk")
            part = CHUNK_GROUPS // W_LOADS
            for j in range(0, CHUNK_GROUPS, part):
                nc.sync.dma_start(
                    out=w_chunk[:, j : j + part, :].bitcast(I32),
                    in_=w_words[:, c * CHUNK_GROUPS + j : c * CHUNK_GROUPS + j + part, :],
                )
            w_of[c] = w_chunk

        def load_a():
            a_sb = const.tile([P, TILES, NODES], BF16)
            nc.sync.dma_start(out=a_sb[:], in_=a_rows)
            rows_of[ITEMS] = a_sb[:].bitcast(F32)

        items_of_round = [list(range(s, min(s + RUN, ITEMS + 1))) for s in range(0, ITEMS + 1, RUN)]
        sorted_of = {}
        grouped_of = {}
        codes_of = {}
        planes_of = {}

        def sort_round(r):
            for item in items_of_round[r]:
                sorted_words = work.tile([P, PACK, HALVES, P], F32, name="sorted_words")
                nc.vector.tensor_copy(
                    out=sorted_words[:], in_=rows_of[item].rearrange("r n (p u) -> r n u p", u=HALVES)
                )
                sorted_of[item] = sorted_words
                if item + X_BUFS < ITEMS:
                    load_item(item + X_BUFS)
                if item + X_BUFS == ITEMS - 1:
                    load_a()

        def transpose_round(r):
            for item in items_of_round[r]:
                grouped = work.tile([P, PACK * P * PACK], BF16, align_bytes=64, name="grouped")
                grouped_words = grouped[:].bitcast(F32).rearrange("p (n r u) -> p n r u", n=PACK, u=HALVES)
                for first in range(0, PACK, 2):
                    bank = bank_pool.tile([P, 2, HALVES, P], F32, name="bank")
                    for i in range(2):
                        for u in range(HALVES):
                            nc.tensor.transpose(bank[:, i, u, :], sorted_of[item][:, first + i, u, :], ident[:])
                    nc.scalar.copy(
                        out=grouped_words[:, first : first + 2, :, :],
                        in_=bank[:].rearrange("p n u r -> p n r u"),
                    )
                grouped_of[item] = grouped

        def quantise_round(r):
            for item in items_of_round[r]:
                codes = work.tile([P, PACK, P], U32, align_bytes=64, name="codes")
                planes = work.tile([P, PACK, P], U8, align_bytes=64, name="planes")
                nc.vector.quantize_mx(
                    out=codes[:].rearrange("p n r -> p (n r)").bitcast(FP8X4),
                    scales=planes[:].rearrange("p n r -> p (n r)"),
                    in_=grouped_of[item][:],
                )
                codes_of[item] = codes
                planes_of[item] = planes

        acc = [acc_pool.tile([P, HID], F32, name="acc%d" % t) for t in range(TILES)]
        h = const.tile([P, TILES, HID], F32)

        def multiply_round(r):
            for item in items_of_round[r]:
                c, t = divmod(item, TILES)
                for j in range(CHUNK_GROUPS):
                    nc.tensor.matmul_mx(
                        out=acc[t][:],
                        lhsT=codes_of[item][:, j, :].bitcast(FP8X4),
                        lhsT_scale=planes_of[item][:, j, :],
                        rhs=w_of[c][:, j, :].bitcast(FP8X4),
                        rhs_scale=w_planes[4 * j : P, c, :],
                        start=(c == 0 and j == 0),
                        stop=(c == CHUNKS - 1 and j == CHUNK_GROUPS - 1),
                    )

        def add_bias_round(r):
            for item in items_of_round[r]:
                c, t = divmod(item, TILES)
                if c == CHUNKS - 1 and t < TILES - 1:
                    nc.vector.tensor_tensor(out=h[:, t, :], in0=acc[t][:], in1=bias[:], op=ADD)

        for item in range(X_BUFS):
            load_item(item)

        nc.sync.dma_start(out=first_row[0:1, 0:HID], in_=b_in.unsqueeze(0))
        nc.sync.dma_start(out=first_row[0:1, HID : HID + 1], in_=eps0.unsqueeze(0))
        bias = const.tile([P, HID], F32)
        one_plus_eps = const.tile([P, 1], F32)

        def spread_constants():
            spread_b = bank_pool.tile([P, HID], F32, name="spread_b", tag="bank")
            nc.tensor.matmul(out=spread_b[:], lhsT=ones[:], rhs=first_row[:, 0:HID], start=True, stop=True)
            spread_eps = bank_pool.tile([P, EPS_COLS], F32, name="spread_eps", tag="bank")
            nc.tensor.matmul(out=spread_eps[:], lhsT=ones[:], rhs=first_row[:, HID:], start=True, stop=True)
            nc.scalar.copy(out=bias[:], in_=spread_b[:])
            nc.vector.tensor_scalar_add(out=one_plus_eps[:], in0=spread_eps[:, 0:1], scalar1=1.0)

        sort_round(0)
        transpose_round(0)
        sort_round(1)
        for r in range(ROUNDS + 1):
            if r + 1 <= ROUNDS:
                transpose_round(r + 1)
            quantise_round(r)
            if r >= 1:
                add_bias_round(r - 1)
            if r + 2 <= ROUNDS:
                sort_round(r + 2)
            if r < ROUNDS:
                multiply_round(r)
            if r == ROUNDS // 2:
                spread_constants()

        h_grouped = const.tile([P, HID, PACK], BF16, align_bytes=64)
        h_by_column = h[:].rearrange("r t n -> r n t")
        h_codes = const.tile([P, HID], U32, align_bytes=64)
        h_planes = const.tile([P, HID], U8, align_bytes=64)
        result = const.tile([P, 2, TILES, HALF], F32)

        def last_bias(wave):
            cols = slice(wave * HALF, (wave + 1) * HALF)
            nc.vector.tensor_tensor(
                out=h[:, TILES - 1, cols], in0=acc[TILES - 1][:, cols], in1=bias[:, cols], op=ADD
            )

        def regroup_h(wave):
            split = wave * HALF + VECTOR_COLS
            nc.vector.tensor_copy(
                out=h_grouped[:, wave * HALF : split, :], in_=h_by_column[:, wave * HALF : split, :]
            )
            nc.scalar.copy(
                out=h_grouped[:, split : (wave + 1) * HALF, :], in_=h_by_column[:, split : (wave + 1) * HALF, :]
            )

        def quantise_h(wave):
            cols = slice(wave * HALF, (wave + 1) * HALF)
            nc.vector.quantize_mx(
                out=h_codes[:, cols].bitcast(FP8X4),
                scales=h_planes[:, cols],
                in_=h_grouped[:, cols, :].rearrange("r n t -> r (n t)"),
            )

        def gather(wave):
            cols = slice(wave * HALF, (wave + 1) * HALF)
            for first in range(0, TILES, 2):
                gathered = bank_pool.tile([P, 2, HALF], F32, name="gathered", tag="bank")
                for i in range(2):
                    nc.tensor.matmul_mx(
                        out=gathered[:, i, :],
                        lhsT=codes_of[ITEMS][:, first + i, :].bitcast(FP8X4),
                        lhsT_scale=planes_of[ITEMS][:, first + i, :],
                        rhs=h_codes[:, cols].bitcast(FP8X4),
                        rhs_scale=h_planes[:, cols],
                        start=True,
                        stop=True,
                    )
                nc.vector.scalar_tensor_tensor(
                    out=result[:, wave, first : first + 2, :],
                    in0=h[:, first : first + 2, cols],
                    scalar=one_plus_eps[:, 0:1],
                    in1=gathered[:],
                    op0=MULT,
                    op1=ADD,
                )
                nc.sync.dma_start(
                    out=out_rows[:, first : first + 2, cols], in_=result[:, wave, first : first + 2, :]
                )

        last_bias(0)
        regroup_h(0)
        last_bias(1)
        quantise_h(0)
        regroup_h(1)
        quantise_h(1)
        gather(0)
        gather(1)
